import numpy as np
import ml_dtypes


def mxq(x, axis, fmt="e4m3"):
    dtype, down = {"e4m3": (ml_dtypes.float8_e4m3fn, 7), "e5m2": (ml_dtypes.float8_e5m2, 14)}[fmt]
    v = np.moveaxis(np.asarray(x, np.float32).astype(ml_dtypes.bfloat16).astype(np.float64), axis, -1)
    blocks = v.reshape(v.shape[:-1] + (-1, 32))
    amax = np.abs(blocks).max(-1, keepdims=True)
    byte = np.maximum(np.where(amax > 0, np.frexp(amax)[1] - 1 + 127, 0) - down, 1)
    scale = np.exp2(byte - 127.0)
    codes = (blocks / scale).astype(np.float32).astype(dtype).astype(np.float64)
    return np.moveaxis((codes * scale).reshape(v.shape), -1, axis)


WIDE = False


def mx_kscale(k):
    if not WIDE:
        return np.ones(k)
    levels = np.array([20, -20, 10, -10, 0])
    a = np.random.permutation(np.resize(levels, k // 512 * 4)).reshape(k // 512, 4)
    idx = np.arange(k)
    return np.exp2(a[idx // 512, idx % 128 // 32])


BF16 = ml_dtypes.bfloat16


def bf(x):
    return np.asarray(x, np.float32).astype(BF16)


def f64(x):
    return np.asarray(x).astype(np.float64)


B, S, IN, OUT, GS = 4, 2048, 1024, 512, 128
G = IN // GS
T = B * S


def setup_inputs():
    s = mx_kscale(T).reshape(B, S, 1)
    quantized_x = np.random.standard_normal((B, S, IN)) * s
    scales_x = 0.25 + 0.75 * np.random.random((B, S, 1))
    weight = np.random.standard_normal((OUT, IN))
    weight_scales = (0.5 + np.random.random((OUT, G))) / np.sqrt(IN)
    offset_w = np.random.standard_normal((OUT, G))
    g = np.random.standard_normal((B, S, OUT)) * np.exp2(np.random.randint(-12, 1, (B, S, 1))) / s
    return {"quantized_x": bf(quantized_x),
            "scales_x": bf(scales_x),
            "weight": bf(weight),
            "weight_scales": bf(weight_scales),
            "offset_w": bf(offset_w),
            "grad_out": bf(g)}


def reference(quantized_x, scales_x, weight, weight_scales, offset_w, grad_out):
    x = (f64(quantized_x) * f64(scales_x)).reshape(T, IN)
    g = f64(grad_out).reshape(T, OUT)
    dW = mxq(g, 0, "e5m2").T @ mxq(x, 0, "e4m3")
    return (dW.reshape(OUT, G, GS) * f64(weight_scales)[:, :, None]).reshape(OUT, IN)

@@ -1,0 +1,192 @@
+from contextlib import ExitStack
+
+import concourse.mybir as mybir
+
+FLOPS = 2 * 8192 * 512 * 1024
+BYTES = 8192 * 1024 * 2 + 8192 * 512 * 2 + 512 * 1024 * 4 + 8192 * 2 + 512 * 8 * 2
+
+BF16 = mybir.dt.bfloat16
+F32 = mybir.dt.float32
+U32 = mybir.dt.uint32
+U8 = mybir.dt.uint8
+E4M3 = mybir.dt.float8_e4m3fn_x4
+E5M2 = mybir.dt.float8_e5m2_x4
+MULT = mybir.AluOpType.mult
+COPY = mybir.ActivationFunctionType.Copy
+
+P = 128
+PACK = 4
+K_PASS = P * PACK
+TOKENS = 8192
+IN = 1024
+OUT = 512
+GS = 128
+N_CHUNKS = TOKENS // K_PASS
+N_TILE = 512
+M_TILES = OUT // P
+N_TILES = IN // N_TILE
+RAW_BUFS = 6
+X_V = 512
+
+
+def regroup_views(dst, src):
+    return (
+        dst.rearrange("p (c i) t -> p c t i", i=4),
+        src.rearrange("p t (c i) -> p c t i", i=4),
+    )
+
+
+def tile_quarotfp16linear_t_kernel(
+    tc, quantized_x, scales_x, weight, weight_scales, offset_w, grad_out, out
+):
+    nc = tc.nc
+    x_view = quantized_x.flatten_outer_dims().rearrange("(c p j) w -> c p j w", p=P, j=PACK)
+    g_view = grad_out.flatten_outer_dims().rearrange("(c p j) w -> c p j w", p=P, j=PACK)
+    s_view = scales_x.flatten_outer_dims().rearrange("(c p j) o -> p c (j o)", p=P, j=PACK)
+    ws_view = weight_scales.rearrange("(m p) g -> p m g", p=P)
+
+    with ExitStack() as ctx:
+        const = ctx.enter_context(tc.tile_pool(name="const", bufs=1))
+        raw = ctx.enter_context(tc.tile_pool(name="raw", bufs=RAW_BUFS))
+        grouped = ctx.enter_context(tc.tile_pool(name="grouped", bufs=3))
+        codes = ctx.enter_context(tc.tile_pool(name="codes", bufs=3))
+        res = ctx.enter_context(tc.tile_pool(name="res", bufs=4))
+        psum = ctx.enter_context(tc.psum_pool(name="acc", bufs=1))
+        ctx.enter_context(tc.manual_schedule())
+
+        s_bf = const.tile([P, N_CHUNKS, PACK], BF16, name="s_bf")
+        s_f = const.tile([P, N_CHUNKS, PACK], F32, name="s_f")
+        ws_bf = const.tile([P, M_TILES, IN // GS], BF16, name="ws_bf")
+        ws_f = const.tile([P, M_TILES, IN // GS], F32, name="ws_f")
+        nc.scalar.dma_start(out=s_bf[:], in_=s_view)
+        nc.scalar.dma_start(out=ws_bf[:], in_=ws_view)
+
+        acc = {}
+        for m in range(M_TILES):
+            for n in range(N_TILES):
+                acc[(m, n)] = psum.tile([P, N_TILE], F32, name="acc%d%d" % (m, n))
+
+        xr = {}
+        gr = {}
+        xg = {}
+        gg = {}
+        xc = {}
+        xp = {}
+        gc = {}
+        gp = {}
+
+        def load(c):
+            gr[c] = raw.tile([P, PACK, OUT], BF16, name="gr")
+            xr[c] = raw.tile([P, PACK, IN], BF16, name="xr")
+            nc.sync.dma_start(out=gr[c][:], in_=g_view[c])
+            nc.sync.dma_start(out=xr[c][:], in_=x_view[c])
+
+        def scale(c):
+            for j in range(PACK):
+                nc.vector.tensor_scalar(
+                    out=xr[c][:, j, :],
+                    in0=xr[c][:, j, :],
+                    scalar1=s_f[:, c, j : j + 1],
+                    scalar2=None,
+                    op0=MULT,
+                )
+
+        def regroup_scalar(c):
+            gg[c] = grouped.tile([P, OUT, PACK], BF16, name="gg", align_bytes=64)
+            xg[c] = grouped.tile([P, IN, PACK], BF16, name="xg", align_bytes=64)
+            dst, src = regroup_views(gg[c][:], gr[c][:])
+            nc.scalar.copy(out=dst, in_=src)
+            dst, src = regroup_views(xg[c][:, X_V:IN, :], xr[c][:, :, X_V:IN])
+            nc.scalar.copy(out=dst, in_=src)
+
+        def regroup_vector(c):
+            dst, src = regroup_views(xg[c][:, 0:X_V, :], xr[c][:, :, 0:X_V])
+            nc.vector.tensor_copy(out=dst, in_=src)
+
+        def quantise_g_x0(c):
+            gc[c] = codes.tile([P, OUT], U32, name="gc", align_bytes=64)
+            gp[c] = codes.tile([P, OUT], U8, name="gp", align_bytes=64)
+            xc[c] = codes.tile([P, IN], U32, name="xc", align_bytes=64)
+            xp[c] = codes.tile([P, IN], U8, name="xp", align_bytes=64)
+            nc.vector.quantize_mx(
+                out=gc[c][:].bitcast(E5M2),
+                scales=gp[c][:],
+                in_=gg[c][:].rearrange("p w j -> p (w j)"),
+            )
+            quantise_x(c, 0)
+
+        def quantise_x(c, n):
+            cols = slice(n * N_TILE, (n + 1) * N_TILE)
+            nc.vector.quantize_mx(
+                out=xc[c][:, cols].bitcast(E4M3),
+                scales=xp[c][:, cols],
+                in_=xg[c][:, cols, :].rearrange("p w j -> p (w j)"),
+            )
+
+        def multiply(c, n):
+            cols = slice(n * N_TILE, (n + 1) * N_TILE)
+            for m in range(M_TILES):
+                rows = slice(m * P, (m + 1) * P)
+                nc.tensor.matmul_mx(
+                    out=acc[(m, n)][:],
+                    lhsT=gc[c][:, rows].bitcast(E5M2),
+                    lhsT_scale=gp[c][:, rows],
+                    rhs=xc[c][:, cols].bitcast(E4M3),
+                    rhs_scale=xp[c][:, cols],
+                    start=(c == 0),
+                    stop=(c == N_CHUNKS - 1),
+                )
+
+        def finish(m, n, on_vector):
+            groups = N_TILE // GS
+            ot = res.tile([P, N_TILE], F32, name="ot")
+            if on_vector:
+                nc.vector.tensor_tensor(
+                    out=ot[:].rearrange("p (g w) -> p g w", g=groups),
+                    in0=acc[(m, n)][:].rearrange("p (g w) -> p g w", g=groups),
+                    in1=ws_f[:, m, n * groups : (n + 1) * groups]
+                    .unsqueeze(2)
+                    .to_broadcast([P, groups, GS]),
+                    op=MULT,
+                )
+            else:
+                for q in range(groups):
+                    k = n * groups + q
+                    nc.scalar.activation(
+                        out=ot[:, q * GS : (q + 1) * GS],
+                        in_=acc[(m, n)][:, q * GS : (q + 1) * GS],
+                        func=COPY,
+                        scale=ws_f[:, m, k : k + 1],
+                    )
+            nc.sync.dma_start(
+                out=out[m * P : (m + 1) * P, n * N_TILE : (n + 1) * N_TILE], in_=ot[:]
+            )
+
+        for c in range(RAW_BUFS):
+            load(c)
+        nc.vector.tensor_copy(out=s_f[:], in_=s_bf[:])
+        for c in range(N_CHUNKS + 1):
+            if c < N_CHUNKS:
+                scale(c)
+                regroup_scalar(c)
+            if c >= 1:
+                quantise_g_x0(c - 1)
+                multiply(c - 1, 0)
+            if c < N_CHUNKS:
+                regroup_vector(c)
+                if c + RAW_BUFS < N_CHUNKS:
+                    load(c + RAW_BUFS)
+            if c == 1:
+                nc.vector.tensor_copy(out=ws_f[:], in_=ws_bf[:])
+            if c >= 1:
+                quantise_x(c - 1, 1)
+                multiply(c - 1, 1)
+
+        finish(0, 0, False)
+        finish(1, 0, False)
+        finish(2, 0, True)
+        finish(3, 0, True)
+        finish(0, 1, False)
+        finish(1, 1, False)
+        finish(2, 1, True)
+        finish(3, 1, True)

@@ -26,7 +26,7 @@ N_TILE = 512
 M_TILES = OUT // P
 N_TILES = IN // N_TILE
 RAW_BUFS = 6
-X_V = 512
+X_V = 576
 
 
 def regroup_views(dst, src):
@@ -50,7 +50,7 @@ def tile_quarotfp16linear_t_kernel(
         raw = ctx.enter_context(tc.tile_pool(name="raw", bufs=RAW_BUFS))
         grouped = ctx.enter_context(tc.tile_pool(name="grouped", bufs=3))
         codes = ctx.enter_context(tc.tile_pool(name="codes", bufs=3))
-        res = ctx.enter_context(tc.tile_pool(name="res", bufs=4))
+        res = ctx.enter_context(tc.tile_pool(name="res", bufs=8))
         psum = ctx.enter_context(tc.psum_pool(name="acc", bufs=1))
         ctx.enter_context(tc.manual_schedule())
 
@@ -79,7 +79,11 @@ def tile_quarotfp16linear_t_kernel(
             gr[c] = raw.tile([P, PACK, OUT], BF16, name="gr")
             xr[c] = raw.tile([P, PACK, IN], BF16, name="xr")
             nc.sync.dma_start(out=gr[c][:], in_=g_view[c])
-            nc.sync.dma_start(out=xr[c][:], in_=x_view[c])
+            if c == 0:
+                for j in range(PACK):
+                    nc.sync.dma_start(out=xr[c][:, j, :], in_=x_view[c][:, j, :])
+            else:
+                nc.sync.dma_start(out=xr[c][:], in_=x_view[c])
 
         def scale(c):
             for j in range(PACK):
@@ -103,36 +107,33 @@ def tile_quarotfp16linear_t_kernel(
             dst, src = regroup_views(xg[c][:, 0:X_V, :], xr[c][:, :, 0:X_V])
             nc.vector.tensor_copy(out=dst, in_=src)
 
-        def quantise_g_x0(c):
+        def quantise_g(c):
             gc[c] = codes.tile([P, OUT], U32, name="gc", align_bytes=64)
             gp[c] = codes.tile([P, OUT], U8, name="gp", align_bytes=64)
-            xc[c] = codes.tile([P, IN], U32, name="xc", align_bytes=64)
-            xp[c] = codes.tile([P, IN], U8, name="xp", align_bytes=64)
             nc.vector.quantize_mx(
                 out=gc[c][:].bitcast(E5M2),
                 scales=gp[c][:],
                 in_=gg[c][:].rearrange("p w j -> p (w j)"),
             )
-            quantise_x(c, 0)
 
         def quantise_x(c, n):
-            cols = slice(n * N_TILE, (n + 1) * N_TILE)
+            xc[(c, n)] = codes.tile([P, N_TILE], U32, name="xc%d" % n, align_bytes=64)
+            xp[(c, n)] = codes.tile([P, N_TILE], U8, name="xp%d" % n, align_bytes=64)
             nc.vector.quantize_mx(
-                out=xc[c][:, cols].bitcast(E4M3),
-                scales=xp[c][:, cols],
-                in_=xg[c][:, cols, :].rearrange("p w j -> p (w j)"),
+                out=xc[(c, n)][:].bitcast(E4M3),
+                scales=xp[(c, n)][:],
+                in_=xg[c][:, n * N_TILE : (n + 1) * N_TILE, :].rearrange("p w j -> p (w j)"),
             )
 
         def multiply(c, n):
-            cols = slice(n * N_TILE, (n + 1) * N_TILE)
             for m in range(M_TILES):
                 rows = slice(m * P, (m + 1) * P)
                 nc.tensor.matmul_mx(
                     out=acc[(m, n)][:],
                     lhsT=gc[c][:, rows].bitcast(E5M2),
                     lhsT_scale=gp[c][:, rows],
-                    rhs=xc[c][:, cols].bitcast(E4M3),
-                    rhs_scale=xp[c][:, cols],
+                    rhs=xc[(c, n)][:].bitcast(E4M3),
+                    rhs_scale=xp[(c, n)][:],
                     start=(c == 0),
                     stop=(c == N_CHUNKS - 1),
                 )
@@ -165,28 +166,31 @@ def tile_quarotfp16linear_t_kernel(
         for c in range(RAW_BUFS):
             load(c)
         nc.vector.tensor_copy(out=s_f[:], in_=s_bf[:])
-        for c in range(N_CHUNKS + 1):
-            if c < N_CHUNKS:
-                scale(c)
-                regroup_scalar(c)
-            if c >= 1:
-                quantise_g_x0(c - 1)
-                multiply(c - 1, 0)
-            if c < N_CHUNKS:
-                regroup_vector(c)
-                if c + RAW_BUFS < N_CHUNKS:
-                    load(c + RAW_BUFS)
-            if c == 1:
+        scale(0)
+        for i in range(N_CHUNKS + 1):
+            if i < N_CHUNKS:
+                regroup_scalar(i)
+            if i >= 1:
+                quantise_g(i - 1)
+                quantise_x(i - 1, 0)
+                multiply(i - 1, 0)
+            if i < N_CHUNKS:
+                regroup_vector(i)
+                if i + RAW_BUFS < N_CHUNKS:
+                    load(i + RAW_BUFS)
+            if i + 1 < N_CHUNKS:
+                scale(i + 1)
+            if i == 1:
                 nc.vector.tensor_copy(out=ws_f[:], in_=ws_bf[:])
-            if c >= 1:
-                quantise_x(c - 1, 1)
-                multiply(c - 1, 1)
+            if i >= 1:
+                quantise_x(i - 1, 1)
+                multiply(i - 1, 1)
 
         finish(0, 0, False)
-        finish(1, 0, False)
         finish(2, 0, True)
         finish(3, 0, True)
-        finish(0, 1, False)
-        finish(1, 1, False)
-        finish(2, 1, True)
+        finish(1, 0, False)
+        finish(0, 1, True)
+        finish(1, 1, True)
+        finish(2, 1, False)
         finish(3, 1, True)

@@ -1,6 +1,7 @@
 from contextlib import ExitStack
 
 import concourse.mybir as mybir
+from concourse.masks import make_identity
 
 FLOPS = 2 * 8192 * 512 * 1024
 BYTES = 8192 * 1024 * 2 + 8192 * 512 * 2 + 512 * 1024 * 4 + 8192 * 2 + 512 * 8 * 2
@@ -25,8 +26,13 @@ N_CHUNKS = TOKENS // K_PASS
 N_TILE = 512
 M_TILES = OUT // P
 N_TILES = IN // N_TILE
-RAW_BUFS = 6
-X_V = 576
+RAW_BUFS = 5
+HELPED = 13
+HB_COLS = 256
+X_V_HELPED = 480
+X_V_PLAIN = 576
+LATE = (3, 1)
+LATE_ROUNDS = 3
 
 
 def regroup_views(dst, src):
@@ -50,6 +56,7 @@ def tile_quarotfp16linear_t_kernel(
         raw = ctx.enter_context(tc.tile_pool(name="raw", bufs=RAW_BUFS))
         grouped = ctx.enter_context(tc.tile_pool(name="grouped", bufs=3))
         codes = ctx.enter_context(tc.tile_pool(name="codes", bufs=3))
+        keep = ctx.enter_context(tc.tile_pool(name="keep", bufs=1))
         res = ctx.enter_context(tc.tile_pool(name="res", bufs=8))
         psum = ctx.enter_context(tc.psum_pool(name="acc", bufs=1))
         ctx.enter_context(tc.manual_schedule())
@@ -58,18 +65,23 @@ def tile_quarotfp16linear_t_kernel(
         s_f = const.tile([P, N_CHUNKS, PACK], F32, name="s_f")
         ws_bf = const.tile([P, M_TILES, IN // GS], BF16, name="ws_bf")
         ws_f = const.tile([P, M_TILES, IN // GS], F32, name="ws_f")
+        ident = const.tile([P, P], BF16, name="ident")
         nc.scalar.dma_start(out=s_bf[:], in_=s_view)
         nc.scalar.dma_start(out=ws_bf[:], in_=ws_view)
+        make_identity(nc, ident[:])
 
         acc = {}
         for m in range(M_TILES):
             for n in range(N_TILES):
-                acc[(m, n)] = psum.tile([P, N_TILE], F32, name="acc%d%d" % (m, n))
+                if (m, n) != LATE:
+                    acc[(m, n)] = psum.tile([P, N_TILE], F32, name="acc%d%d" % (m, n))
+        opened = set()
 
         xr = {}
         gr = {}
         xg = {}
         gg = {}
+        hb = {}
         xc = {}
         xp = {}
         gc = {}
@@ -78,11 +90,14 @@ def tile_quarotfp16linear_t_kernel(
         def load(c):
             gr[c] = raw.tile([P, PACK, OUT], BF16, name="gr")
             xr[c] = raw.tile([P, PACK, IN], BF16, name="xr")
-            nc.sync.dma_start(out=gr[c][:], in_=g_view[c])
             if c == 0:
-                for j in range(PACK):
+                nc.sync.dma_start(out=gr[c][:, :, HB_COLS:OUT], in_=g_view[c][:, :, HB_COLS:OUT])
+                nc.sync.dma_start(out=xr[c][:, 0, :], in_=x_view[c][:, 0, :])
+                nc.sync.dma_start(out=gr[c][:, :, 0:HB_COLS], in_=g_view[c][:, :, 0:HB_COLS])
+                for j in range(1, PACK):
                     nc.sync.dma_start(out=xr[c][:, j, :], in_=x_view[c][:, j, :])
             else:
+                nc.sync.dma_start(out=gr[c][:], in_=g_view[c])
                 nc.sync.dma_start(out=xr[c][:], in_=x_view[c])
 
         def scale(c):
@@ -95,21 +110,48 @@ def tile_quarotfp16linear_t_kernel(
                     op0=MULT,
                 )
 
+        def x_v(c):
+            return X_V_HELPED if c < HELPED else X_V_PLAIN
+
+        def interleave_g(c):
+            hb[c] = psum.tile([P, HB_COLS, PACK], BF16, name="late")
+            for pair in range(PACK // 2):
+                odd = gr[c][:, 2 * pair + 1, 0:HB_COLS]
+                nc.tensor.matmul(
+                    out=hb[c][:, :, 2 * pair : 2 * pair + 2],
+                    lhsT=ident[:],
+                    rhs=odd.unsqueeze(2).to_broadcast([P, HB_COLS, 2]),
+                    start=True,
+                    stop=True,
+                )
+                nc.tensor.matmul(
+                    out=hb[c][:, :, 2 * pair],
+                    lhsT=ident[:],
+                    rhs=gr[c][:, 2 * pair, 0:HB_COLS],
+                    start=True,
+                    stop=True,
+                )
+
         def regroup_scalar(c):
             gg[c] = grouped.tile([P, OUT, PACK], BF16, name="gg", align_bytes=64)
             xg[c] = grouped.tile([P, IN, PACK], BF16, name="xg", align_bytes=64)
-            dst, src = regroup_views(gg[c][:], gr[c][:])
+            first = HB_COLS if c < HELPED else 0
+            dst, src = regroup_views(gg[c][:, first:OUT, :], gr[c][:, :, first:OUT])
             nc.scalar.copy(out=dst, in_=src)
-            dst, src = regroup_views(xg[c][:, X_V:IN, :], xr[c][:, :, X_V:IN])
+            if c < HELPED:
+                nc.scalar.copy(out=gg[c][:, 0:HB_COLS, :], in_=hb[c][:])
+            dst, src = regroup_views(xg[c][:, x_v(c) : IN, :], xr[c][:, :, x_v(c) : IN])
             nc.scalar.copy(out=dst, in_=src)
 
         def regroup_vector(c):
-            dst, src = regroup_views(xg[c][:, 0:X_V, :], xr[c][:, :, 0:X_V])
+            dst, src = regroup_views(xg[c][:, 0 : x_v(c), :], xr[c][:, :, 0 : x_v(c)])
             nc.vector.tensor_copy(out=dst, in_=src)
 
         def quantise_g(c):
-            gc[c] = codes.tile([P, OUT], U32, name="gc", align_bytes=64)
-            gp[c] = codes.tile([P, OUT], U8, name="gp", align_bytes=64)
+            pool = keep if c < HELPED else codes
+            tail = "%d" % c if c < HELPED else ""
+            gc[c] = pool.tile([P, OUT], U32, name="gc" + tail, align_bytes=64)
+            gp[c] = pool.tile([P, OUT], U8, name="gp" + tail, align_bytes=64)
             nc.vector.quantize_mx(
                 out=gc[c][:].bitcast(E5M2),
                 scales=gp[c][:],
@@ -117,26 +159,43 @@ def tile_quarotfp16linear_t_kernel(
             )
 
         def quantise_x(c, n):
-            xc[(c, n)] = codes.tile([P, N_TILE], U32, name="xc%d" % n, align_bytes=64)
-            xp[(c, n)] = codes.tile([P, N_TILE], U8, name="xp%d" % n, align_bytes=64)
+            kept = n == LATE[1] and c < HELPED
+            pool = keep if kept else codes
+            tail = "%d" % n + ("_%d" % c if kept else "")
+            xc[(c, n)] = pool.tile([P, N_TILE], U32, name="xc" + tail, align_bytes=64)
+            xp[(c, n)] = pool.tile([P, N_TILE], U8, name="xp" + tail, align_bytes=64)
             nc.vector.quantize_mx(
                 out=xc[(c, n)][:].bitcast(E4M3),
                 scales=xp[(c, n)][:],
                 in_=xg[c][:, n * N_TILE : (n + 1) * N_TILE, :].rearrange("p w j -> p (w j)"),
             )
 
+        def one_pass(c, m, n):
+            rows = slice(m * P, (m + 1) * P)
+            nc.tensor.matmul_mx(
+                out=acc[(m, n)][:],
+                lhsT=gc[c][:, rows].bitcast(E5M2),
+                lhsT_scale=gp[c][:, rows],
+                rhs=xc[(c, n)][:].bitcast(E4M3),
+                rhs_scale=xp[(c, n)][:],
+                start=((m, n) not in opened),
+                stop=(c == N_CHUNKS - 1),
+            )
+            opened.add((m, n))
+
         def multiply(c, n):
             for m in range(M_TILES):
-                rows = slice(m * P, (m + 1) * P)
-                nc.tensor.matmul_mx(
-                    out=acc[(m, n)][:],
-                    lhsT=gc[c][:, rows].bitcast(E5M2),
-                    lhsT_scale=gp[c][:, rows],
-                    rhs=xc[(c, n)][:].bitcast(E4M3),
-                    rhs_scale=xp[(c, n)][:],
-                    start=(c == 0),
-                    stop=(c == N_CHUNKS - 1),
-                )
+                if c >= HELPED or (m, n) != LATE:
+                    one_pass(c, m, n)
+
+        def first_half(c):
+            quantise_g(c)
+            quantise_x(c, 0)
+            multiply(c, 0)
+
+        def second_half(c):
+            quantise_x(c, 1)
+            multiply(c, 1)
 
         def finish(m, n, on_vector):
             groups = N_TILE // GS
@@ -163,32 +222,43 @@ def tile_quarotfp16linear_t_kernel(
                 out=out[m * P : (m + 1) * P, n * N_TILE : (n + 1) * N_TILE], in_=ot[:]
             )
 
+        late_todo = list(range(HELPED))
+        late_per_round = (HELPED + LATE_ROUNDS - 1) // LATE_ROUNDS
+
         for c in range(RAW_BUFS):
             load(c)
         nc.vector.tensor_copy(out=s_f[:], in_=s_bf[:])
         scale(0)
-        for i in range(N_CHUNKS + 1):
-            if i < N_CHUNKS:
-                regroup_scalar(i)
+        interleave_g(0)
+        last = N_CHUNKS - 1
+        for i in range(N_CHUNKS):
+            regroup_scalar(i)
             if i >= 1:
-                quantise_g(i - 1)
-                quantise_x(i - 1, 0)
-                multiply(i - 1, 0)
-            if i < N_CHUNKS:
-                regroup_vector(i)
-                if i + RAW_BUFS < N_CHUNKS:
-                    load(i + RAW_BUFS)
-            if i + 1 < N_CHUNKS:
+                first_half(i - 1)
+            if i + 1 < HELPED:
+                interleave_g(i + 1)
+            if i + 1 == HELPED:
+                acc[LATE] = psum.tile([P, N_TILE], F32, name="late")
+            regroup_vector(i)
+            if i + RAW_BUFS < N_CHUNKS:
+                load(i + RAW_BUFS)
+            if i < last:
                 scale(i + 1)
+            else:
+                first_half(i)
             if i == 1:
                 nc.vector.tensor_copy(out=ws_f[:], in_=ws_bf[:])
             if i >= 1:
-                quantise_x(i - 1, 1)
-                multiply(i - 1, 1)
+                second_half(i - 1)
+            if i > last - LATE_ROUNDS:
+                for c in late_todo[0:late_per_round]:
+                    one_pass(c, LATE[0], LATE[1])
+                late_todo = late_todo[late_per_round:]
+        second_half(last)
 
         finish(0, 0, False)
-        finish(2, 0, True)
         finish(3, 0, True)
+        finish(2, 0, True)
         finish(1, 0, False)
         finish(0, 1, True)
         finish(1, 1, True)

@@ -27,12 +27,12 @@ N_TILE = 512
 M_TILES = OUT // P
 N_TILES = IN // N_TILE
 RAW_BUFS = 5
-HELPED = 13
+HELPED = 12
 HB_COLS = 256
-X_V_HELPED = 480
-X_V_PLAIN = 576
-LATE = (3, 1)
-LATE_ROUNDS = 3
+X_V_HELPED = 376
+X_V_PLAIN = 544
+LATE = ((2, 1), (3, 1))
+LATE_ROUNDS = 4
 
 
 def regroup_views(dst, src):
@@ -73,7 +73,7 @@ def tile_quarotfp16linear_t_kernel(
         acc = {}
         for m in range(M_TILES):
             for n in range(N_TILES):
-                if (m, n) != LATE:
+                if (m, n) not in LATE:
                     acc[(m, n)] = psum.tile([P, N_TILE], F32, name="acc%d%d" % (m, n))
         opened = set()
 
@@ -91,9 +91,9 @@ def tile_quarotfp16linear_t_kernel(
             gr[c] = raw.tile([P, PACK, OUT], BF16, name="gr")
             xr[c] = raw.tile([P, PACK, IN], BF16, name="xr")
             if c == 0:
-                nc.sync.dma_start(out=gr[c][:, :, HB_COLS:OUT], in_=g_view[c][:, :, HB_COLS:OUT])
-                nc.sync.dma_start(out=xr[c][:, 0, :], in_=x_view[c][:, 0, :])
                 nc.sync.dma_start(out=gr[c][:, :, 0:HB_COLS], in_=g_view[c][:, :, 0:HB_COLS])
+                nc.sync.dma_start(out=xr[c][:, 0, :], in_=x_view[c][:, 0, :])
+                nc.sync.dma_start(out=gr[c][:, :, HB_COLS:OUT], in_=g_view[c][:, :, HB_COLS:OUT])
                 for j in range(1, PACK):
                     nc.sync.dma_start(out=xr[c][:, j, :], in_=x_view[c][:, j, :])
             else:
@@ -114,32 +114,44 @@ def tile_quarotfp16linear_t_kernel(
             return X_V_HELPED if c < HELPED else X_V_PLAIN
 
         def interleave_g(c):
-            hb[c] = psum.tile([P, HB_COLS, PACK], BF16, name="late")
-            for pair in range(PACK // 2):
-                odd = gr[c][:, 2 * pair + 1, 0:HB_COLS]
-                nc.tensor.matmul(
-                    out=hb[c][:, :, 2 * pair : 2 * pair + 2],
-                    lhsT=ident[:],
-                    rhs=odd.unsqueeze(2).to_broadcast([P, HB_COLS, 2]),
-                    start=True,
-                    stop=True,
+            hb[c] = []
+            for b in range(len(LATE)):
+                bank = psum.tile([P, HB_COLS, PACK], BF16, name="late%d" % b)
+                words = (
+                    bank[:]
+                    .rearrange("p w j -> p (w j)")
+                    .bitcast(F32)
+                    .rearrange("p (w a) -> p w a", a=PACK // 2)
                 )
-                nc.tensor.matmul(
-                    out=hb[c][:, :, 2 * pair],
-                    lhsT=ident[:],
-                    rhs=gr[c][:, 2 * pair, 0:HB_COLS],
-                    start=True,
-                    stop=True,
-                )
+                cols = slice(b * HB_COLS, (b + 1) * HB_COLS)
+                for a in range(PACK // 2):
+                    nc.tensor.matmul(
+                        out=words[:, :, a],
+                        lhsT=ident[:],
+                        rhs=gr[c][:, 2 * a + 1, cols],
+                        start=True,
+                        stop=True,
+                    )
+                    nc.tensor.matmul(
+                        out=bank[:, :, 2 * a],
+                        lhsT=ident[:],
+                        rhs=gr[c][:, 2 * a, cols],
+                        start=True,
+                        stop=True,
+                    )
+                hb[c].append(bank)
 
         def regroup_scalar(c):
             gg[c] = grouped.tile([P, OUT, PACK], BF16, name="gg", align_bytes=64)
             xg[c] = grouped.tile([P, IN, PACK], BF16, name="xg", align_bytes=64)
-            first = HB_COLS if c < HELPED else 0
-            dst, src = regroup_views(gg[c][:, first:OUT, :], gr[c][:, :, first:OUT])
-            nc.scalar.copy(out=dst, in_=src)
             if c < HELPED:
-                nc.scalar.copy(out=gg[c][:, 0:HB_COLS, :], in_=hb[c][:])
+                for b in range(len(LATE)):
+                    nc.scalar.copy(
+                        out=gg[c][:, b * HB_COLS : (b + 1) * HB_COLS, :], in_=hb[c][b][:]
+                    )
+            else:
+                dst, src = regroup_views(gg[c][:], gr[c][:])
+                nc.scalar.copy(out=dst, in_=src)
             dst, src = regroup_views(xg[c][:, x_v(c) : IN, :], xr[c][:, :, x_v(c) : IN])
             nc.scalar.copy(out=dst, in_=src)
 
@@ -159,7 +171,7 @@ def tile_quarotfp16linear_t_kernel(
             )
 
         def quantise_x(c, n):
-            kept = n == LATE[1] and c < HELPED
+            kept = n == 1 and c < HELPED
             pool = keep if kept else codes
             tail = "%d" % n + ("_%d" % c if kept else "")
             xc[(c, n)] = pool.tile([P, N_TILE], U32, name="xc" + tail, align_bytes=64)
@@ -185,7 +197,7 @@ def tile_quarotfp16linear_t_kernel(
 
         def multiply(c, n):
             for m in range(M_TILES):
-                if c >= HELPED or (m, n) != LATE:
+                if c >= HELPED or (m, n) not in LATE:
                     one_pass(c, m, n)
 
         def first_half(c):
@@ -233,12 +245,13 @@ def tile_quarotfp16linear_t_kernel(
         last = N_CHUNKS - 1
         for i in range(N_CHUNKS):
             regroup_scalar(i)
-            if i >= 1:
-                first_half(i - 1)
             if i + 1 < HELPED:
                 interleave_g(i + 1)
             if i + 1 == HELPED:
-                acc[LATE] = psum.tile([P, N_TILE], F32, name="late")
+                for b in range(len(LATE)):
+                    acc[LATE[b]] = psum.tile([P, N_TILE], F32, name="late%d" % b)
+            if i >= 1:
+                first_half(i - 1)
             regroup_vector(i)
             if i + RAW_BUFS < N_CHUNKS:
                 load(i + RAW_BUFS)
@@ -252,7 +265,8 @@ def tile_quarotfp16linear_t_kernel(
                 second_half(i - 1)
             if i > last - LATE_ROUNDS:
                 for c in late_todo[0:late_per_round]:
-                    one_pass(c, LATE[0], LATE[1])
+                    for m, n in LATE:
+                        one_pass(c, m, n)
                 late_todo = late_todo[late_per_round:]
         second_half(last)
 

@@ -26,7 +26,7 @@ N_CHUNKS = TOKENS // K_PASS
 N_TILE = 512
 M_TILES = OUT // P
 N_TILES = IN // N_TILE
-RAW_BUFS = 5
+RAW_BUFS = 6
 HELPED = 12
 HB_COLS = 256
 X_V_HELPED = 376
@@ -66,6 +66,9 @@ def tile_quarotfp16linear_t_kernel(
         ws_bf = const.tile([P, M_TILES, IN // GS], BF16, name="ws_bf")
         ws_f = const.tile([P, M_TILES, IN // GS], F32, name="ws_f")
         ident = const.tile([P, P], BF16, name="ident")
+        s0_bf = const.tile([P, PACK], BF16, name="s0_bf")
+        s0_f = const.tile([P, PACK], F32, name="s0_f")
+        nc.sync.dma_start(out=s0_bf[:], in_=s_view[:, 0, :])
         nc.scalar.dma_start(out=s_bf[:], in_=s_view)
         nc.scalar.dma_start(out=ws_bf[:], in_=ws_view)
         make_identity(nc, ident[:])
@@ -105,7 +108,7 @@ def tile_quarotfp16linear_t_kernel(
                 nc.vector.tensor_scalar(
                     out=xr[c][:, j, :],
                     in0=xr[c][:, j, :],
-                    scalar1=s_f[:, c, j : j + 1],
+                    scalar1=(s0_f[:, j : j + 1] if c == 0 else s_f[:, c, j : j + 1]),
                     scalar2=None,
                     op0=MULT,
                 )
@@ -239,7 +242,7 @@ def tile_quarotfp16linear_t_kernel(
 
         for c in range(RAW_BUFS):
             load(c)
-        nc.vector.tensor_copy(out=s_f[:], in_=s_bf[:])
+        nc.vector.tensor_copy(out=s0_f[:], in_=s0_bf[:])
         scale(0)
         interleave_g(0)
         last = N_CHUNKS - 1
@@ -255,6 +258,8 @@ def tile_quarotfp16linear_t_kernel(
             regroup_vector(i)
             if i + RAW_BUFS < N_CHUNKS:
                 load(i + RAW_BUFS)
+            if i == 0:
+                nc.vector.tensor_copy(out=s_f[:], in_=s_bf[:])
             if i < last:
                 scale(i + 1)
             else:
@@ -263,7 +268,7 @@ def tile_quarotfp16linear_t_kernel(
                 nc.vector.tensor_copy(out=ws_f[:], in_=ws_bf[:])
             if i >= 1:
                 second_half(i - 1)
-            if i > last - LATE_ROUNDS:
+            if i + 1 >= HELPED:
                 for c in late_todo[0:late_per_round]:
                     for m, n in LATE:
                         one_pass(c, m, n)

@@ -119,24 +119,18 @@ def tile_quarotfp16linear_t_kernel(
         def interleave_g(c):
             hb[c] = []
             for b in range(len(LATE)):
-                bank = psum.tile([P, HB_COLS, PACK], BF16, name="late%d" % b)
-                words = (
-                    bank[:]
-                    .rearrange("p w j -> p (w j)")
-                    .bitcast(F32)
-                    .rearrange("p (w a) -> p w a", a=PACK // 2)
-                )
+                bank = psum.tile([P, PACK // 2, HB_COLS], F32, name="late%d" % b)
                 cols = slice(b * HB_COLS, (b + 1) * HB_COLS)
                 for a in range(PACK // 2):
                     nc.tensor.matmul(
-                        out=words[:, :, a],
+                        out=bank[:, a, :],
                         lhsT=ident[:],
                         rhs=gr[c][:, 2 * a + 1, cols],
                         start=True,
                         stop=True,
                     )
                     nc.tensor.matmul(
-                        out=bank[:, :, 2 * a],
+                        out=bank[:, a, :].bitcast(BF16).rearrange("p (w e) -> p w e", e=2)[:, :, 0],
                         lhsT=ident[:],
                         rhs=gr[c][:, 2 * a, cols],
                         start=True,
@@ -150,7 +144,11 @@ def tile_quarotfp16linear_t_kernel(
             if c < HELPED:
                 for b in range(len(LATE)):
                     nc.scalar.copy(
-                        out=gg[c][:, b * HB_COLS : (b + 1) * HB_COLS, :], in_=hb[c][b][:]
+                        out=gg[c][:, b * HB_COLS : (b + 1) * HB_COLS, :]
+                        .rearrange("p w j -> p (w j)")
+                        .bitcast(F32)
+                        .rearrange("p (w a) -> p w a", a=PACK // 2),
+                        in_=hb[c][b][:].rearrange("p a w -> p w a"),
                     )
             else:
                 dst, src = regroup_views(gg[c][:], gr[c][:])

@@ -29,7 +29,8 @@ N_TILES = IN // N_TILE
 RAW_BUFS = 6
 HELPED = 12
 HB_COLS = 256
-X_V_HELPED = 376
+RUN = 8
+X_V_HELPED = 384
 X_V_PLAIN = 544
 LATE = ((2, 1), (3, 1))
 LATE_ROUNDS = 4
@@ -37,8 +38,8 @@ LATE_ROUNDS = 4
 
 def regroup_views(dst, src):
     return (
-        dst.rearrange("p (c i) t -> p c t i", i=4),
-        src.rearrange("p t (c i) -> p c t i", i=4),
+        dst.rearrange("p (c i) t -> p c t i", i=RUN),
+        src.rearrange("p t (c i) -> p c t i", i=RUN),
     )
 
 

@@ -26,14 +26,16 @@ N_CHUNKS = TOKENS // K_PASS
 N_TILE = 512
 M_TILES = OUT // P
 N_TILES = IN // N_TILE
-RAW_BUFS = 6
-HELPED = 12
+RAW_BUFS = 5
+HELP_FROM, HELP_TO = 1, 12
 HB_COLS = 256
 RUN = 8
+X_V_FIRST = 256
 X_V_HELPED = 384
 X_V_PLAIN = 544
+SPLIT = 3
 LATE = ((2, 1), (3, 1))
-LATE_ROUNDS = 4
+LATE_PER_ROUND = 4
 
 
 def regroup_views(dst, src):
@@ -51,6 +53,8 @@ def tile_quarotfp16linear_t_kernel(
     g_view = grad_out.flatten_outer_dims().rearrange("(c p j) w -> c p j w", p=P, j=PACK)
     s_view = scales_x.flatten_outer_dims().rearrange("(c p j) o -> p c (j o)", p=P, j=PACK)
     ws_view = weight_scales.rearrange("(m p) g -> p m g", p=P)
+    scalar_copy = nc.scalar.copy
+    vector_copy = nc.vector.tensor_copy
 
     with ExitStack() as ctx:
         const = ctx.enter_context(tc.tile_pool(name="const", bufs=1))
@@ -69,7 +73,7 @@ def tile_quarotfp16linear_t_kernel(
         ident = const.tile([P, P], BF16, name="ident")
         s0_bf = const.tile([P, PACK], BF16, name="s0_bf")
         s0_f = const.tile([P, PACK], F32, name="s0_f")
-        nc.sync.dma_start(out=s0_bf[:], in_=s_view[:, 0, :])
+        nc.scalar.dma_start(out=s0_bf[:], in_=s_view[:, 0, :])
         nc.scalar.dma_start(out=s_bf[:], in_=s_view)
         nc.scalar.dma_start(out=ws_bf[:], in_=ws_view)
         make_identity(nc, ident[:])
@@ -91,18 +95,20 @@ def tile_quarotfp16linear_t_kernel(
         gc = {}
         gp = {}
 
+        def load_g(c, lo, hi):
+            nc.sync.dma_start(out=gr[c][:, :, lo:hi], in_=g_view[c][:, :, lo:hi])
+
         def load(c):
             gr[c] = raw.tile([P, PACK, OUT], BF16, name="gr")
             xr[c] = raw.tile([P, PACK, IN], BF16, name="xr")
+            load_g(c, 0, HB_COLS if c == 0 else OUT)
+            step = 1 if c == 0 else 2 if c < SPLIT else PACK
+            for j in range(0, PACK, step):
+                nc.sync.dma_start(
+                    out=xr[c][:, j : j + step, :], in_=x_view[c][:, j : j + step, :]
+                )
             if c == 0:
-                nc.sync.dma_start(out=gr[c][:, :, 0:HB_COLS], in_=g_view[c][:, :, 0:HB_COLS])
-                nc.sync.dma_start(out=xr[c][:, 0, :], in_=x_view[c][:, 0, :])
-                nc.sync.dma_start(out=gr[c][:, :, HB_COLS:OUT], in_=g_view[c][:, :, HB_COLS:OUT])
-                for j in range(1, PACK):
-                    nc.sync.dma_start(out=xr[c][:, j, :], in_=x_view[c][:, j, :])
-            else:
-                nc.sync.dma_start(out=gr[c][:], in_=g_view[c])
-                nc.sync.dma_start(out=xr[c][:], in_=x_view[c])
+                load_g(c, HB_COLS, OUT)
 
         def scale(c):
             for j in range(PACK):
@@ -114,8 +120,13 @@ def tile_quarotfp16linear_t_kernel(
                     op0=MULT,
                 )
 
+        def helped(c):
+            return HELP_FROM <= c < HELP_TO
+
         def x_v(c):
-            return X_V_HELPED if c < HELPED else X_V_PLAIN
+            if c == 0:
+                return X_V_FIRST
+            return X_V_HELPED if helped(c) else X_V_PLAIN
 
         def interleave_g(c):
             hb[c] = []
@@ -139,59 +150,54 @@ def tile_quarotfp16linear_t_kernel(
                     )
                 hb[c].append(bank)
 
-        def regroup_scalar(c):
+        def open_chunk(c):
             gg[c] = grouped.tile([P, OUT, PACK], BF16, name="gg", align_bytes=64)
             xg[c] = grouped.tile([P, IN, PACK], BF16, name="xg", align_bytes=64)
-            if c < HELPED:
-                for b in range(len(LATE)):
-                    nc.scalar.copy(
-                        out=gg[c][:, b * HB_COLS : (b + 1) * HB_COLS, :]
-                        .rearrange("p w j -> p (w j)")
-                        .bitcast(F32)
-                        .rearrange("p (w a) -> p w a", a=PACK // 2),
-                        in_=hb[c][b][:].rearrange("p a w -> p w a"),
-                    )
-            else:
-                dst, src = regroup_views(gg[c][:], gr[c][:])
-                nc.scalar.copy(out=dst, in_=src)
-            dst, src = regroup_views(xg[c][:, x_v(c) : IN, :], xr[c][:, :, x_v(c) : IN])
-            nc.scalar.copy(out=dst, in_=src)
-
-        def regroup_vector(c):
-            dst, src = regroup_views(xg[c][:, 0 : x_v(c), :], xr[c][:, :, 0 : x_v(c)])
-            nc.vector.tensor_copy(out=dst, in_=src)
-
-        def quantise_g(c):
-            pool = keep if c < HELPED else codes
-            tail = "%d" % c if c < HELPED else ""
+            kept = c < HELP_TO
+            pool = keep if kept else codes
+            tail = "%d" % c if kept else ""
             gc[c] = pool.tile([P, OUT], U32, name="gc" + tail, align_bytes=64)
             gp[c] = pool.tile([P, OUT], U8, name="gp" + tail, align_bytes=64)
+            xc[c] = pool.tile([P, IN], U32, name="xc" + tail, align_bytes=64)
+            xp[c] = pool.tile([P, IN], U8, name="xp" + tail, align_bytes=64)
+
+        def regroup(copy, grouped_tile, raw_tile, lo, hi):
+            dst, src = regroup_views(grouped_tile[:, lo:hi, :], raw_tile[:, :, lo:hi])
+            copy(out=dst, in_=src)
+
+        def drain_g(c):
+            for b in range(len(LATE)):
+                nc.scalar.copy(
+                    out=gg[c][:, b * HB_COLS : (b + 1) * HB_COLS, :]
+                    .rearrange("p w j -> p (w j)")
+                    .bitcast(F32)
+                    .rearrange("p (w a) -> p w a", a=PACK // 2),
+                    in_=hb[c][b][:].rearrange("p a w -> p w a"),
+                )
+
+        def quantise_g(c):
             nc.vector.quantize_mx(
                 out=gc[c][:].bitcast(E5M2),
                 scales=gp[c][:],
                 in_=gg[c][:].rearrange("p w j -> p (w j)"),
             )
 
-        def quantise_x(c, n):
-            kept = n == 1 and c < HELPED
-            pool = keep if kept else codes
-            tail = "%d" % n + ("_%d" % c if kept else "")
-            xc[(c, n)] = pool.tile([P, N_TILE], U32, name="xc" + tail, align_bytes=64)
-            xp[(c, n)] = pool.tile([P, N_TILE], U8, name="xp" + tail, align_bytes=64)
+        def quantise_x(c, lo, hi):
             nc.vector.quantize_mx(
-                out=xc[(c, n)][:].bitcast(E4M3),
-                scales=xp[(c, n)][:],
-                in_=xg[c][:, n * N_TILE : (n + 1) * N_TILE, :].rearrange("p w j -> p (w j)"),
+                out=xc[c][:, lo:hi].bitcast(E4M3),
+                scales=xp[c][:, lo:hi],
+                in_=xg[c][:, lo:hi, :].rearrange("p w j -> p (w j)"),
             )
 
         def one_pass(c, m, n):
             rows = slice(m * P, (m + 1) * P)
+            cols = slice(n * N_TILE, (n + 1) * N_TILE)
             nc.tensor.matmul_mx(
                 out=acc[(m, n)][:],
                 lhsT=gc[c][:, rows].bitcast(E5M2),
                 lhsT_scale=gp[c][:, rows],
-                rhs=xc[(c, n)][:].bitcast(E4M3),
-                rhs_scale=xp[(c, n)][:],
+                rhs=xc[c][:, cols].bitcast(E4M3),
+                rhs_scale=xp[c][:, cols],
                 start=((m, n) not in opened),
                 stop=(c == N_CHUNKS - 1),
             )
@@ -199,17 +205,12 @@ def tile_quarotfp16linear_t_kernel(
 
         def multiply(c, n):
             for m in range(M_TILES):
-                if c >= HELPED or (m, n) not in LATE:
+                if c >= HELP_TO or (m, n) not in LATE:
                     one_pass(c, m, n)
 
-        def first_half(c):
-            quantise_g(c)
-            quantise_x(c, 0)
-            multiply(c, 0)
-
-        def second_half(c):
-            quantise_x(c, 1)
-            multiply(c, 1)
+        def quantise_and_multiply_half(c, n):
+            quantise_x(c, n * N_TILE, (n + 1) * N_TILE)
+            multiply(c, n)
 
         def finish(m, n, on_vector):
             groups = N_TILE // GS
@@ -236,48 +237,65 @@ def tile_quarotfp16linear_t_kernel(
                 out=out[m * P : (m + 1) * P, n * N_TILE : (n + 1) * N_TILE], in_=ot[:]
             )
 
-        late_todo = list(range(HELPED))
-        late_per_round = (HELPED + LATE_ROUNDS - 1) // LATE_ROUNDS
+        late_todo = list(range(HELP_TO))
+        last = N_CHUNKS - 1
 
         for c in range(RAW_BUFS):
             load(c)
-        nc.vector.tensor_copy(out=s0_f[:], in_=s0_bf[:])
+        vector_copy(out=s0_f[:], in_=s0_bf[:])
         scale(0)
-        interleave_g(0)
-        last = N_CHUNKS - 1
-        for i in range(N_CHUNKS):
-            regroup_scalar(i)
-            if i + 1 < HELPED:
+
+        open_chunk(0)
+        regroup(scalar_copy, gg[0], gr[0], 0, HB_COLS)
+        regroup(scalar_copy, xg[0], xr[0], X_V_FIRST, IN)
+        interleave_g(1)
+        regroup(vector_copy, xg[0], xr[0], 0, X_V_FIRST)
+        regroup(vector_copy, gg[0], gr[0], HB_COLS, OUT)
+        load(RAW_BUFS)
+        quantise_g(0)
+        vector_copy(out=s_f[:], in_=s_bf[:])
+        scale(1)
+
+        for i in range(1, N_CHUNKS):
+            open_chunk(i)
+            if helped(i):
+                drain_g(i)
+            else:
+                regroup(scalar_copy, gg[i], gr[i], 0, OUT)
+            regroup(scalar_copy, xg[i], xr[i], x_v(i), IN)
+            if helped(i + 1):
                 interleave_g(i + 1)
-            if i + 1 == HELPED:
+            if i + 1 == HELP_TO:
                 for b in range(len(LATE)):
                     acc[LATE[b]] = psum.tile([P, N_TILE], F32, name="late%d" % b)
-            if i >= 1:
-                first_half(i - 1)
-            regroup_vector(i)
+            if i > 1:
+                quantise_g(i - 1)
+            if i == last:
+                quantise_and_multiply_half(i - 1, 0)
+            regroup(vector_copy, xg[i], xr[i], 0, x_v(i))
             if i + RAW_BUFS < N_CHUNKS:
                 load(i + RAW_BUFS)
-            if i == 0:
-                nc.vector.tensor_copy(out=s_f[:], in_=s_bf[:])
             if i < last:
+                quantise_x(i - 1, 0, IN)
+                for n in range(N_TILES):
+                    multiply(i - 1, n)
                 scale(i + 1)
-            else:
-                first_half(i)
             if i == 1:
-                nc.vector.tensor_copy(out=ws_f[:], in_=ws_bf[:])
-            if i >= 1:
-                second_half(i - 1)
-            if i + 1 >= HELPED:
-                for c in late_todo[0:late_per_round]:
+                vector_copy(out=ws_f[:], in_=ws_bf[:])
+            if i + 1 >= HELP_TO:
+                for c in late_todo[0:LATE_PER_ROUND]:
                     for m, n in LATE:
                         one_pass(c, m, n)
-                late_todo = late_todo[late_per_round:]
-        second_half(last)
+                late_todo = late_todo[LATE_PER_ROUND:]
 
-        finish(0, 0, False)
-        finish(3, 0, True)
-        finish(2, 0, True)
+        quantise_g(last)
+        quantise_and_multiply_half(last, 0)
+        quantise_and_multiply_half(last - 1, 1)
+        finish(0, 0, True)
+        quantise_and_multiply_half(last, 1)
         finish(1, 0, False)
+        finish(2, 0, True)
+        finish(3, 0, False)
         finish(0, 1, True)
         finish(1, 1, True)
         finish(2, 1, False)

@@ -156,10 +156,10 @@ def tile_quarotfp16linear_t_kernel(
             kept = c < HELP_TO
             pool = keep if kept else codes
             tail = "%d" % c if kept else ""
-            gc[c] = pool.tile([P, OUT], U32, name="gc" + tail, align_bytes=64)
-            gp[c] = pool.tile([P, OUT], U8, name="gp" + tail, align_bytes=64)
-            xc[c] = pool.tile([P, IN], U32, name="xc" + tail, align_bytes=64)
-            xp[c] = pool.tile([P, IN], U8, name="xp" + tail, align_bytes=64)
+            gc[c] = pool.tile([P, OUT], U32, name="gc" + tail, align_bytes=256)
+            gp[c] = pool.tile([P, OUT], U8, name="gp" + tail, align_bytes=256)
+            xc[c] = pool.tile([P, IN], U32, name="xc" + tail, align_bytes=256)
+            xp[c] = pool.tile([P, IN], U8, name="xp" + tail, align_bytes=256)
 
         def regroup(copy, grouped_tile, raw_tile, lo, hi):
             dst, src = regroup_views(grouped_tile[:, lo:hi, :], raw_tile[:, :, lo:hi])
@@ -249,11 +249,11 @@ def tile_quarotfp16linear_t_kernel(
         regroup(scalar_copy, gg[0], gr[0], 0, HB_COLS)
         regroup(scalar_copy, xg[0], xr[0], X_V_FIRST, IN)
         interleave_g(1)
-        regroup(vector_copy, xg[0], xr[0], 0, X_V_FIRST)
+        vector_copy(out=s_f[:], in_=s_bf[:])
         regroup(vector_copy, gg[0], gr[0], HB_COLS, OUT)
+        regroup(vector_copy, xg[0], xr[0], 0, X_V_FIRST)
         load(RAW_BUFS)
         quantise_g(0)
-        vector_copy(out=s_f[:], in_=s_bf[:])
         scale(1)
 
         for i in range(1, N_CHUNKS):
@@ -268,6 +268,11 @@ def tile_quarotfp16linear_t_kernel(
             if i + 1 == HELP_TO:
                 for b in range(len(LATE)):
                     acc[LATE[b]] = psum.tile([P, N_TILE], F32, name="late%d" % b)
+            if i + 1 >= HELP_TO:
+                for c in late_todo[0:LATE_PER_ROUND]:
+                    for m, n in LATE:
+                        one_pass(c, m, n)
+                late_todo = late_todo[LATE_PER_ROUND:]
             if i > 1:
                 quantise_g(i - 1)
             if i == last:
@@ -282,11 +287,6 @@ def tile_quarotfp16linear_t_kernel(
                 scale(i + 1)
             if i == 1:
                 vector_copy(out=ws_f[:], in_=ws_bf[:])
-            if i + 1 >= HELP_TO:
-                for c in late_todo[0:LATE_PER_ROUND]:
-                    for m, n in LATE:
-                        one_pass(c, m, n)
-                late_todo = late_todo[LATE_PER_ROUND:]
 
         quantise_g(last)
         quantise_and_multiply_half(last, 0)

from contextlib import ExitStack

import concourse.mybir as mybir
from concourse.masks import make_identity

FLOPS = 2 * 8192 * 512 * 1024
BYTES = 8192 * 1024 * 2 + 8192 * 512 * 2 + 512 * 1024 * 4 + 8192 * 2 + 512 * 8 * 2

BF16 = mybir.dt.bfloat16
F32 = mybir.dt.float32
U32 = mybir.dt.uint32
U8 = mybir.dt.uint8
E4M3 = mybir.dt.float8_e4m3fn_x4
E5M2 = mybir.dt.float8_e5m2_x4
MULT = mybir.AluOpType.mult
COPY = mybir.ActivationFunctionType.Copy

P = 128
PACK = 4
K_PASS = P * PACK
TOKENS = 8192
IN = 1024
OUT = 512
GS = 128
N_CHUNKS = TOKENS // K_PASS
N_TILE = 512
M_TILES = OUT // P
N_TILES = IN // N_TILE
RAW_BUFS = 5
HELP_FROM, HELP_TO = 1, 12
HB_COLS = 256
RUN = 8
X_V_FIRST = 256
X_V_HELPED = 384
X_V_PLAIN = 544
SPLIT = 3
LATE = ((2, 1), (3, 1))
LATE_PER_ROUND = 4


def regroup_views(dst, src):
    return (
        dst.rearrange("p (c i) t -> p c t i", i=RUN),
        src.rearrange("p t (c i) -> p c t i", i=RUN),
    )


def tile_quarotfp16linear_t_kernel(
    tc, quantized_x, scales_x, weight, weight_scales, offset_w, grad_out, out
):
    nc = tc.nc
    x_view = quantized_x.flatten_outer_dims().rearrange("(c p j) w -> c p j w", p=P, j=PACK)
    g_view = grad_out.flatten_outer_dims().rearrange("(c p j) w -> c p j w", p=P, j=PACK)
    s_view = scales_x.flatten_outer_dims().rearrange("(c p j) o -> p c (j o)", p=P, j=PACK)
    ws_view = weight_scales.rearrange("(m p) g -> p m g", p=P)
    scalar_copy = nc.scalar.copy
    vector_copy = nc.vector.tensor_copy

    with ExitStack() as ctx:
        const = ctx.enter_context(tc.tile_pool(name="const", bufs=1))
        raw = ctx.enter_context(tc.tile_pool(name="raw", bufs=RAW_BUFS))
        grouped = ctx.enter_context(tc.tile_pool(name="grouped", bufs=3))
        codes = ctx.enter_context(tc.tile_pool(name="codes", bufs=3))
        keep = ctx.enter_context(tc.tile_pool(name="keep", bufs=1))
        res = ctx.enter_context(tc.tile_pool(name="res", bufs=8))
        psum = ctx.enter_context(tc.psum_pool(name="acc", bufs=1))
        ctx.enter_context(tc.manual_schedule())

        s_bf = const.tile([P, N_CHUNKS, PACK], BF16, name="s_bf")
        s_f = const.tile([P, N_CHUNKS, PACK], F32, name="s_f")
        ws_bf = const.tile([P, M_TILES, IN // GS], BF16, name="ws_bf")
        ws_f = const.tile([P, M_TILES, IN // GS], F32, name="ws_f")
        ident = const.tile([P, P], BF16, name="ident")
        s0_bf = const.tile([P, PACK], BF16, name="s0_bf")
        s0_f = const.tile([P, PACK], F32, name="s0_f")
        nc.scalar.dma_start(out=s0_bf[:], in_=s_view[:, 0, :])
        nc.scalar.dma_start(out=s_bf[:], in_=s_view)
        nc.scalar.dma_start(out=ws_bf[:], in_=ws_view)
        make_identity(nc, ident[:])

        acc = {}
        for m in range(M_TILES):
            for n in range(N_TILES):
                if (m, n) not in LATE:
                    acc[(m, n)] = psum.tile([P, N_TILE], F32, name="acc%d%d" % (m, n))
        opened = set()

        xr = {}
        gr = {}
        xg = {}
        gg = {}
        hb = {}
        xc = {}
        xp = {}
        gc = {}
        gp = {}

        def load_g(c, lo, hi):
            nc.sync.dma_start(out=gr[c][:, :, lo:hi], in_=g_view[c][:, :, lo:hi])

        def load(c):
            gr[c] = raw.tile([P, PACK, OUT], BF16, name="gr")
            xr[c] = raw.tile([P, PACK, IN], BF16, name="xr")
            load_g(c, 0, HB_COLS if c == 0 else OUT)
            step = 1 if c == 0 else 2 if c < SPLIT else PACK
            for j in range(0, PACK, step):
                nc.sync.dma_start(
                    out=xr[c][:, j : j + step, :], in_=x_view[c][:, j : j + step, :]
                )
            if c == 0:
                load_g(c, HB_COLS, OUT)

        def scale(c):
            for j in range(PACK):
                nc.vector.tensor_scalar(
                    out=xr[c][:, j, :],
                    in0=xr[c][:, j, :],
                    scalar1=(s0_f[:, j : j + 1] if c == 0 else s_f[:, c, j : j + 1]),
                    scalar2=None,
                    op0=MULT,
                )

        def helped(c):
            return HELP_FROM <= c < HELP_TO

        def x_v(c):
            if c == 0:
                return X_V_FIRST
            return X_V_HELPED if helped(c) else X_V_PLAIN

        def interleave_g(c):
            hb[c] = []
            for b in range(len(LATE)):
                bank = psum.tile([P, PACK // 2, HB_COLS], F32, name="late%d" % b)
                cols = slice(b * HB_COLS, (b + 1) * HB_COLS)
                for a in range(PACK // 2):
                    nc.tensor.matmul(
                        out=bank[:, a, :],
                        lhsT=ident[:],
                        rhs=gr[c][:, 2 * a + 1, cols],
                        start=True,
                        stop=True,
                    )
                    nc.tensor.matmul(
                        out=bank[:, a, :].bitcast(BF16).rearrange("p (w e) -> p w e", e=2)[:, :, 0],
                        lhsT=ident[:],
                        rhs=gr[c][:, 2 * a, cols],
                        start=True,
                        stop=True,
                    )
                hb[c].append(bank)

        def open_chunk(c):
            gg[c] = grouped.tile([P, OUT, PACK], BF16, name="gg", align_bytes=64)
            xg[c] = grouped.tile([P, IN, PACK], BF16, name="xg", align_bytes=64)
            kept = c < HELP_TO
            pool = keep if kept else codes
            tail = "%d" % c if kept else ""
            gc[c] = pool.tile([P, OUT], U32, name="gc" + tail, align_bytes=256)
            gp[c] = pool.tile([P, OUT], U8, name="gp" + tail, align_bytes=256)
            xc[c] = pool.tile([P, IN], U32, name="xc" + tail, align_bytes=256)
            xp[c] = pool.tile([P, IN], U8, name="xp" + tail, align_bytes=256)

        def regroup(copy, grouped_tile, raw_tile, lo, hi):
            dst, src = regroup_views(grouped_tile[:, lo:hi, :], raw_tile[:, :, lo:hi])
            copy(out=dst, in_=src)

        def drain_g(c):
            for b in range(len(LATE)):
                nc.scalar.copy(
                    out=gg[c][:, b * HB_COLS : (b + 1) * HB_COLS, :]
                    .rearrange("p w j -> p (w j)")
                    .bitcast(F32)
                    .rearrange("p (w a) -> p w a", a=PACK // 2),
                    in_=hb[c][b][:].rearrange("p a w -> p w a"),
                )

        def quantise_g(c):
            nc.vector.quantize_mx(
                out=gc[c][:].bitcast(E5M2),
                scales=gp[c][:],
                in_=gg[c][:].rearrange("p w j -> p (w j)"),
            )

        def quantise_x(c, lo, hi):
            nc.vector.quantize_mx(
                out=xc[c][:, lo:hi].bitcast(E4M3),
                scales=xp[c][:, lo:hi],
                in_=xg[c][:, lo:hi, :].rearrange("p w j -> p (w j)"),
            )

        def one_pass(c, m, n):
            rows = slice(m * P, (m + 1) * P)
            cols = slice(n * N_TILE, (n + 1) * N_TILE)
            nc.tensor.matmul_mx(
                out=acc[(m, n)][:],
                lhsT=gc[c][:, rows].bitcast(E5M2),
                lhsT_scale=gp[c][:, rows],
                rhs=xc[c][:, cols].bitcast(E4M3),
                rhs_scale=xp[c][:, cols],
                start=((m, n) not in opened),
                stop=(c == N_CHUNKS - 1),
            )
            opened.add((m, n))

        def multiply(c, n):
            for m in range(M_TILES):
                if c >= HELP_TO or (m, n) not in LATE:
                    one_pass(c, m, n)

        def quantise_and_multiply_half(c, n):
            quantise_x(c, n * N_TILE, (n + 1) * N_TILE)
            multiply(c, n)

        def finish(m, n, on_vector):
            groups = N_TILE // GS
            ot = res.tile([P, N_TILE], F32, name="ot")
            if on_vector:
                nc.vector.tensor_tensor(
                    out=ot[:].rearrange("p (g w) -> p g w", g=groups),
                    in0=acc[(m, n)][:].rearrange("p (g w) -> p g w", g=groups),
                    in1=ws_f[:, m, n * groups : (n + 1) * groups]
                    .unsqueeze(2)
                    .to_broadcast([P, groups, GS]),
                    op=MULT,
                )
            else:
                for q in range(groups):
                    k = n * groups + q
                    nc.scalar.activation(
                        out=ot[:, q * GS : (q + 1) * GS],
                        in_=acc[(m, n)][:, q * GS : (q + 1) * GS],
                        func=COPY,
                        scale=ws_f[:, m, k : k + 1],
                    )
            nc.sync.dma_start(
                out=out[m * P : (m + 1) * P, n * N_TILE : (n + 1) * N_TILE], in_=ot[:]
            )

        late_todo = list(range(HELP_TO))
        last = N_CHUNKS - 1

        for c in range(RAW_BUFS):
            load(c)
        vector_copy(out=s0_f[:], in_=s0_bf[:])
        scale(0)

        open_chunk(0)
        regroup(scalar_copy, gg[0], gr[0], 0, HB_COLS)
        regroup(scalar_copy, xg[0], xr[0], X_V_FIRST, IN)
        interleave_g(1)
        vector_copy(out=s_f[:], in_=s_bf[:])
        regroup(vector_copy, gg[0], gr[0], HB_COLS, OUT)
        regroup(vector_copy, xg[0], xr[0], 0, X_V_FIRST)
        load(RAW_BUFS)
        quantise_g(0)
        scale(1)

        for i in range(1, N_CHUNKS):
            open_chunk(i)
            if helped(i):
                drain_g(i)
            else:
                regroup(scalar_copy, gg[i], gr[i], 0, OUT)
            regroup(scalar_copy, xg[i], xr[i], x_v(i), IN)
            if helped(i + 1):
                interleave_g(i + 1)
            if i + 1 == HELP_TO:
                for b in range(len(LATE)):
                    acc[LATE[b]] = psum.tile([P, N_TILE], F32, name="late%d" % b)
            if i + 1 >= HELP_TO:
                for c in late_todo[0:LATE_PER_ROUND]:
                    for m, n in LATE:
                        one_pass(c, m, n)
                late_todo = late_todo[LATE_PER_ROUND:]
            if i > 1:
                quantise_g(i - 1)
            if i == last:
                quantise_and_multiply_half(i - 1, 0)
            regroup(vector_copy, xg[i], xr[i], 0, x_v(i))
            if i + RAW_BUFS < N_CHUNKS:
                load(i + RAW_BUFS)
            if i < last:
                quantise_x(i - 1, 0, IN)
                for n in range(N_TILES):
                    multiply(i - 1, n)
                scale(i + 1)
            if i == 1:
                vector_copy(out=ws_f[:], in_=ws_bf[:])

        quantise_g(last)
        quantise_and_multiply_half(last, 0)
        quantise_and_multiply_half(last - 1, 1)
        finish(0, 0, True)
        quantise_and_multiply_half(last, 1)
        finish(1, 0, False)
        finish(2, 0, True)
        finish(3, 0, False)
        finish(0, 1, True)
        finish(1, 1, True)
        finish(2, 1, False)
        finish(3, 1, True)
